import numpy as np
import ml_dtypes


def mxq(x, axis, fmt="e4m3"):
    dtype, down = {"e4m3": (ml_dtypes.float8_e4m3fn, 7), "e5m2": (ml_dtypes.float8_e5m2, 14)}[fmt]
    v = np.moveaxis(np.asarray(x, np.float32).astype(ml_dtypes.bfloat16).astype(np.float64), axis, -1)
    blocks = v.reshape(v.shape[:-1] + (-1, 32))
    amax = np.abs(blocks).max(-1, keepdims=True)
    byte = np.maximum(np.where(amax > 0, np.frexp(amax)[1] - 1 + 127, 0) - down, 1)
    scale = np.exp2(byte - 127.0)
    codes = (blocks / scale).astype(np.float32).astype(dtype).astype(np.float64)
    return np.moveaxis((codes * scale).reshape(v.shape), -1, axis)


WIDE = False


def mx_kscale(k):
    if not WIDE:
        return np.ones(k)
    levels = np.array([10, -10, 5, -5, 0])
    a = np.random.permutation(np.resize(levels, k // 512 * 4)).reshape(k // 512, 4)
    idx = np.arange(k)
    return np.exp2(a[idx // 512, idx % 128 // 32])


BF16 = ml_dtypes.bfloat16


def bf(x):
    return np.asarray(x, np.float32).astype(BF16)


def f64(x):
    return np.asarray(x).astype(np.float64)


B, D, S, N = 4096, 1024, 2, 128
DS = D // S


def sigmoid(v):
    return 1.0 / (1.0 + np.exp(-v))


def setup_inputs():
    s = mx_kscale(D)
    t = np.maximum(1.0 + 2.0 * np.random.standard_normal((B, N, S)), 0.0) + np.maximum(1.0 + 2.0 * np.random.standard_normal((B, N, S)), 0.0)
    return {"a": bf(t * t / (t * t).sum(axis=1, keepdims=True)),
            "vr": bf(np.random.standard_normal((N, S, DS)) * 0.5 * np.sqrt(N) * s.reshape(S, DS)),
            "h": bf(np.random.standard_normal((B, D)) * s),
            "x2g": bf(np.random.standard_normal((B, D))),
            "w_g": bf(np.random.standard_normal((D, D)) / np.sqrt(D) / s),
            "b_g": bf(np.random.standard_normal(D) * 0.3),
            "bg": bf(1.0 + 0.1 * np.random.standard_normal(1))}


def reference(a, vr, h, x2g, w_g, b_g, bg):
    hf = f64(h)
    hh = (f64(a).transpose(2, 0, 1) @ f64(vr).transpose(1, 0, 2)).transpose(1, 0, 2).reshape(B, D)
    h2g = (mxq(hf, 1, "e4m3") @ mxq(f64(w_g), 1, "e4m3").T) + f64(b_g)
    g = sigmoid(f64(x2g) + h2g + f64(bg))
    return g * hh + (1.0 - g) * hf

@@ -1,0 +1,245 @@
+from contextlib import ExitStack
+
+import concourse.mybir as mybir
+from concourse.masks import make_identity
+
+F32 = mybir.dt.float32
+BF16 = mybir.dt.bfloat16
+U32 = mybir.dt.uint32
+U8 = mybir.dt.uint8
+FP8X4 = mybir.dt.float8_e4m3fn_x4
+ALU = mybir.AluOpType
+ACT = mybir.ActivationFunctionType
+
+P = 128
+B, D, S, N = 4096, 1024, 2, 128
+DS = D // S
+ROWS = 4
+GROUPS = B // (P * ROWS)
+NT = GROUPS * ROWS
+P0_AHEAD = 3
+
+FLOPS = 2 * B * D * D + 2 * B * N * D
+
+
+def is_x(r):
+    return r % 2 == 0
+
+
+def tile_tpru_pb_t_kernel(tc, a, vr, h, x2g, w_g, b_g, bg, out):
+    nc = tc.nc
+    h_v = h.rearrange("(q p i) k -> q p i k", p=P, i=ROWS)
+    x_v = x2g.rearrange("(q p i) k -> q p i k", p=P, i=ROWS)
+    a_v = a.rearrange("(q p i) n s -> q p i (n s)", p=P, i=ROWS)
+    o_v = out.rearrange("(q p i) k -> q p i k", p=P, i=ROWS)
+    w_v = w_g.rearrange("(j p) k -> p j k", p=P)
+
+    with ExitStack() as ctx:
+        const = ctx.enter_context(tc.tile_pool(name="const", bufs=1))
+        ld = ctx.enter_context(tc.tile_pool(name="ld", bufs=3))
+        work = ctx.enter_context(tc.tile_pool(name="work", bufs=3))
+        psum = ctx.enter_context(tc.psum_pool(name="psum", bufs=2))
+        psb = ctx.enter_context(tc.psum_pool(name="psb", bufs=1))
+
+        h_sb, x_sb, a_sb, aT_sb = {}, {}, {}, {}
+        hc_sb, hs_sb, acc_ps, hh_ps, z_sb, o_sb = {}, {}, {}, {}, {}, {}
+
+        def load_x(q):
+            x_sb[q] = ld.tile([P, ROWS, D], BF16, name="x_t", tag="x")
+            nc.sync.dma_start(out=x_sb[q][:], in_=x_v[q])
+
+        def load_h(q):
+            h_sb[q] = ld.tile([P, ROWS, D], BF16, name="h_t", tag="h", bufs=4)
+            nc.sync.dma_start(out=h_sb[q][:], in_=h_v[q])
+
+        def load_a(q):
+            a_sb[q] = ld.tile([P, ROWS, 2 * N], BF16, name="a_t", tag="a")
+            nc.sync.dma_start(out=a_sb[q][:], in_=a_v[q])
+
+        ident_f = const.tile([P, P], F32, name="ident_f")
+        make_identity(nc, ident_f[:])
+        ident_b = const.tile([P, P], BF16, name="ident_b")
+        make_identity(nc, ident_b[:])
+        neg_i = const.tile([P, P], BF16, name="neg_i")
+        nc.vector.tensor_scalar_mul(out=neg_i[:], in0=ident_b[:], scalar1=-1.0)
+
+        brow = const.tile([P, P], BF16, name="brow")
+        nc.vector.memset(brow[:], 0.0)
+        nc.sync.dma_start(out=brow[0:8, :], in_=b_g.rearrange("(j c) -> j c", c=P))
+        bg_b = const.tile([P, 1], BF16, name="bg_b")
+        nc.sync.dma_start(out=bg_b[:], in_=bg.partition_broadcast(P))
+
+        load_x(0)
+        wraw = const.tile([P, 8, D], BF16, name="wraw")
+        nc.sync.dma_start(out=wraw[:, 0:4, :], in_=w_v[:, 0:4, :])
+        load_h(0)
+        load_a(0)
+        vr_sb = const.tile([P, S, DS], BF16, name="vr_sb")
+        nc.sync.dma_start(out=vr_sb[:], in_=vr)
+        nc.sync.dma_start(out=wraw[:, 4:8, :], in_=w_v[:, 4:8, :])
+        load_x(1)
+        load_h(1)
+        load_a(1)
+
+        b_t = psum.tile([P, P], BF16, name="b_t", tag="tp")
+        nc.tensor.transpose(b_t[:], brow[:], ident_b[:])
+        bg_f = const.tile([P, 1], F32, name="bg_f")
+        nc.vector.tensor_copy(out=bg_f[:], in_=bg_b[:])
+        bcol = const.tile([P, 8], F32, name="bcol")
+        nc.vector.tensor_scalar_add(out=bcol[:], in0=b_t[:, 0:8], scalar1=bg_f[:, 0:1])
+        brep = const.tile([P, 8, P], F32, name="brep")
+        nc.vector.tensor_copy(out=brep[:], in_=bcol[:].unsqueeze(2).to_broadcast([P, 8, P]))
+        bias_ps = []
+        for u in range(2):
+            bias_ps.append(psb.tile([P, DS], F32, name="bias%d" % u))
+        for j in range(8):
+            nc.tensor.transpose(bias_ps[j // 4][:, P * (j % 4) : P * (j % 4) + P], brep[:, j, :], ident_f[:])
+
+        def p0(r):
+            q, i = divmod(r, ROWS)
+            z_sb[r] = work.tile([P, D], F32, name="z_t", tag="z", bufs=6)
+            for u in range(2):
+                c = slice(DS * u, DS * u + DS)
+                nc.vector.tensor_tensor(out=z_sb[r][:, c], in0=bias_ps[u][:], in1=x_sb[q][:, i, c], op=ALU.add)
+
+        def aprep(q):
+            tpa = psum.tile([P, ROWS, P], F32, name="tpa", tag="tp")
+            for i in range(ROWS):
+                nc.tensor.transpose(tpa[:, i, :], a_sb[q][:, i, :].bitcast(F32), ident_f[:])
+            aT_sb[q] = work.tile([P, ROWS, S, P], BF16, name="aT", tag="aT", bufs=2)
+            nc.scalar.copy(
+                out=aT_sb[q][:],
+                in_=tpa[:].rearrange("p i b -> p (i b)").bitcast(BF16).rearrange("p (i b s) -> p i s b", i=ROWS, b=P, s=S),
+            )
+
+        def front(r):
+            q, i = divmod(r, ROWS)
+            tph = psum.tile([P, 4, P], F32, name="tph", tag="tp")
+            hw = h_sb[q][:, i, :].bitcast(F32)
+            for blk in range(4):
+                nc.tensor.transpose(tph[:, blk, :], hw[:, P * blk : P * blk + P], ident_f[:])
+            hg = work.tile([P, D], BF16, name="hg", tag="hg", align_bytes=64)
+            nc.scalar.copy(
+                out=hg[:].bitcast(F32).rearrange("p (g r u) -> p g r u", g=2, r=P, u=2),
+                in_=tph[:].rearrange("p (g u) r -> p g r u", g=2, u=2),
+            )
+            hc_sb[r] = work.tile([P, 2, P], U32, name="hc", tag="hc", align_bytes=64)
+            hs_sb[r] = work.tile([P, 2, P], U8, name="hs", tag="hs", align_bytes=64)
+            nc.vector.quantize_mx(
+                out=hc_sb[r][:].rearrange("p g r -> p (g r)").bitcast(FP8X4),
+                scales=hs_sb[r][:].rearrange("p g r -> p (g r)"),
+                in_=hg[:],
+            )
+
+        def mm(r):
+            acc_ps[r] = []
+            for u in range(2):
+                c = slice(DS * u, DS * u + DS)
+                acc = psum.tile([P, DS], F32, name="acc", tag="h2g")
+                for g in range(2):
+                    nc.tensor.matmul_mx(
+                        out=acc[:],
+                        lhsT=hc_sb[r][:, g, :].bitcast(FP8X4),
+                        lhsT_scale=hs_sb[r][:, g, :],
+                        rhs=wc[:, g, c].bitcast(FP8X4),
+                        rhs_scale=ws[:, g, c],
+                        start=(g == 0),
+                        stop=(g == 1),
+                    )
+                acc_ps[r].append(acc)
+
+        def hh(r):
+            q, i = divmod(r, ROWS)
+            hh_ps[r] = []
+            for s in range(S):
+                c = slice(DS * s, DS * s + DS)
+                hb = psum.tile([P, DS], F32, name="hb", tag="hh")
+                nc.tensor.matmul(out=hb[:], lhsT=aT_sb[q][:, i, s, :], rhs=vr_sb[:, s, :], start=True, stop=not is_x(r))
+                if is_x(r):
+                    nc.tensor.matmul(out=hb[:], lhsT=neg_i[:], rhs=h_sb[q][:, i, c], start=False, stop=True)
+                hh_ps[r].append(hb)
+            o_sb[r] = work.tile([P, D], F32, name="o_t", tag="o", bufs=8)
+
+        def p3(r):
+            q, i = divmod(r, ROWS)
+            for s in range(S):
+                c = slice(DS * s, DS * s + DS)
+                nc.vector.tensor_tensor(out=o_sb[r][:, c], in0=hh_ps[r][s][:], in1=h_sb[q][:, i, c], op=ALU.subtract)
+
+        def p1(r):
+            for u in range(2):
+                c = slice(DS * u, DS * u + DS)
+                nc.vector.tensor_tensor(out=z_sb[r][:, c], in0=acc_ps[r][u][:], in1=z_sb[r][:, c], op=ALU.add)
+            nc.scalar.activation(out=z_sb[r][:], in_=z_sb[r][:], func=ACT.Sigmoid)
+
+        def p4x(r):
+            for s in range(S):
+                c = slice(DS * s, DS * s + DS)
+                nc.vector.tensor_tensor(out=o_sb[r][:, c], in0=hh_ps[r][s][:], in1=z_sb[r][:, c], op=ALU.mult)
+
+        def finish(r):
+            q, i = divmod(r, ROWS)
+            if not is_x(r):
+                nc.gpsimd.tensor_tensor(out=o_sb[r][:], in0=o_sb[r][:], in1=z_sb[r][:], op=ALU.mult)
+            nc.gpsimd.tensor_tensor(out=o_sb[r][:], in0=o_sb[r][:], in1=h_sb[q][:, i, :], op=ALU.add)
+            nc.sync.dma_start(out=o_v[q][:, i, :], in_=o_sb[r][:])
+
+        for r in range(P0_AHEAD + 1):
+            p0(r)
+
+        wg = const.tile([P, 2 * D * 4], BF16, name="wg", align_bytes=64)
+        wg_f = wg[:].bitcast(F32).rearrange("p (g c u) -> p g c u", g=2, c=D, u=2)
+        wg_q = wg[:].rearrange("p (g x) -> p g x", g=2)
+        wc = const.tile([P, 2, D], U32, name="wc", align_bytes=64)
+        ws = const.tile([P, 2, D], U8, name="ws", align_bytes=64)
+        for j in range(8):
+            tpw = psum.tile([P, 4, P], F32, name="tpw", tag="tp")
+            wj = wraw[:, j, :].bitcast(F32)
+            for blk in range(4):
+                nc.tensor.transpose(tpw[:, blk, :], wj[:, P * blk : P * blk + P], ident_f[:])
+            src = tpw[:].rearrange("p (g u) r -> p g r u", g=2, u=2)
+            dst = wg_f[:, :, P * j : P * j + P, :]
+            if j % 2 == 0:
+                nc.scalar.copy(out=dst, in_=src)
+            else:
+                nc.vector.tensor_copy(out=dst, in_=src)
+            if j == 3:
+                front(0)
+            if j % 4 == 3:
+                u = j // 4
+                for g in range(2):
+                    nc.vector.quantize_mx(
+                        out=wc[:, g, DS * u : DS * u + DS].bitcast(FP8X4),
+                        scales=ws[:, g, DS * u : DS * u + DS],
+                        in_=wg_q[:, g, 4 * DS * u : 4 * DS * u + 4 * DS],
+                    )
+
+        aprep(0)
+        front(1)
+        mm(0)
+        hh(0)
+        if not is_x(0):
+            p3(0)
+
+        for r in range(NT):
+            q, i = divmod(r, ROWS)
+            if i == 0 and q + 2 < GROUPS:
+                load_x(q + 2)
+                load_h(q + 2)
+                load_a(q + 2)
+            if i == 2 and q + 1 < GROUPS:
+                aprep(q + 1)
+            if r + 2 < NT:
+                front(r + 2)
+            p1(r)
+            if r + 1 < NT:
+                mm(r + 1)
+            if r + 1 + P0_AHEAD < NT:
+                p0(r + 1 + P0_AHEAD)
+            if is_x(r):
+                p4x(r)
+            if r + 1 < NT:
+                hh(r + 1)
+                if not is_x(r + 1):
+                    p3(r + 1)
+            finish(r)

@@ -17,13 +17,17 @@ DS = D // S
 ROWS = 4
 GROUPS = B // (P * ROWS)
 NT = GROUPS * ROWS
-P0_AHEAD = 3
+P0_AHEAD = 5
 
 FLOPS = 2 * B * D * D + 2 * B * N * D
 
 
 def is_x(r):
     return r % 2 == 0
+
+
+def p0_on_gpsimd(r):
+    return r % 3 == 0
 
 
 def tile_tpru_pb_t_kernel(tc, a, vr, h, x2g, w_g, b_g, bg, out):
@@ -42,7 +46,7 @@ def tile_tpru_pb_t_kernel(tc, a, vr, h, x2g, w_g, b_g, bg, out):
         psb = ctx.enter_context(tc.psum_pool(name="psb", bufs=1))
 
         h_sb, x_sb, a_sb, aT_sb = {}, {}, {}, {}
-        hc_sb, hs_sb, acc_ps, hh_ps, z_sb, o_sb = {}, {}, {}, {}, {}, {}
+        hc_sb, hs_sb, acc_ps, hh_ps, z_sb, o_sb, nh_sb = {}, {}, {}, {}, {}, {}, {}
 
         def load_x(q):
             x_sb[q] = ld.tile([P, ROWS, D], BF16, name="x_t", tag="x")
@@ -72,11 +76,18 @@ def tile_tpru_pb_t_kernel(tc, a, vr, h, x2g, w_g, b_g, bg, out):
         load_x(0)
         wraw = const.tile([P, 8, D], BF16, name="wraw")
         nc.sync.dma_start(out=wraw[:, 0:4, :], in_=w_v[:, 0:4, :])
-        load_h(0)
+        h_sb[0] = ld.tile([P, ROWS, D], BF16, name="h_t", tag="h", bufs=4)
+        nc.sync.dma_start(out=h_sb[0][:, 0:1, :], in_=h_v[0][:, 0:1, :])
+        nc.sync.dma_start(out=wraw[:, 4:8, :], in_=w_v[:, 4:8, :])
         load_a(0)
         vr_sb = const.tile([P, S, DS], BF16, name="vr_sb")
         nc.sync.dma_start(out=vr_sb[:], in_=vr)
-        nc.sync.dma_start(out=wraw[:, 4:8, :], in_=w_v[:, 4:8, :])
+        nc.sync.dma_start(out=h_sb[0][:, 1:4, :], in_=h_v[0][:, 1:4, :])
+        vrp_sb = const.tile([P, S, DS], BF16, name="vrp_sb")
+        nc.vector.tensor_copy(
+            out=vrp_sb[:].rearrange("n s (j e p) -> n (s j) e p", j=2, e=2, p=P),
+            in_=vr_sb[:].rearrange("n s (j p e) -> n (s j) e p", j=2, e=2, p=P),
+        )
         load_x(1)
         load_h(1)
         load_a(1)
@@ -95,9 +106,16 @@ def tile_tpru_pb_t_kernel(tc, a, vr, h, x2g, w_g, b_g, bg, out):
         for j in range(8):
             nc.tensor.transpose(bias_ps[j // 4][:, P * (j % 4) : P * (j % 4) + P], brep[:, j, :], ident_f[:])
 
+        bias_sb = const.tile([P, D], F32, name="bias_sb")
+        for u in range(2):
+            nc.scalar.copy(out=bias_sb[:, DS * u : DS * u + DS], in_=bias_ps[u][:])
+
         def p0(r):
             q, i = divmod(r, ROWS)
-            z_sb[r] = work.tile([P, D], F32, name="z_t", tag="z", bufs=6)
+            z_sb[r] = work.tile([P, D], F32, name="z_t", tag="z", bufs=8)
+            if p0_on_gpsimd(r):
+                nc.gpsimd.tensor_tensor(out=z_sb[r][:], in0=x_sb[q][:, i, :], in1=bias_sb[:], op=ALU.add)
+                return
             for u in range(2):
                 c = slice(DS * u, DS * u + DS)
                 nc.vector.tensor_tensor(out=z_sb[r][:, c], in0=bias_ps[u][:], in1=x_sb[q][:, i, c], op=ALU.add)
@@ -123,6 +141,13 @@ def tile_tpru_pb_t_kernel(tc, a, vr, h, x2g, w_g, b_g, bg, out):
                 out=hg[:].bitcast(F32).rearrange("p (g r u) -> p g r u", g=2, r=P, u=2),
                 in_=tph[:].rearrange("p (g u) r -> p g r u", g=2, u=2),
             )
+            if not is_x(r):
+                nh_sb[r] = work.tile([P, 4, 2, P], F32, name="nh", tag="nh", bufs=3)
+                nc.scalar.mul(
+                    out=nh_sb[r][:],
+                    in_=tph[:].rearrange("p j r -> p (j r)").bitcast(BF16).rearrange("p (j r e) -> p j e r", j=4, r=P, e=2),
+                    mul=-1.0,
+                )
             hc_sb[r] = work.tile([P, 2, P], U32, name="hc", tag="hc", align_bytes=64)
             hs_sb[r] = work.tile([P, 2, P], U8, name="hs", tag="hs", align_bytes=64)
             nc.vector.quantize_mx(
@@ -154,17 +179,22 @@ def tile_tpru_pb_t_kernel(tc, a, vr, h, x2g, w_g, b_g, bg, out):
             for s in range(S):
                 c = slice(DS * s, DS * s + DS)
                 hb = psum.tile([P, DS], F32, name="hb", tag="hh")
-                nc.tensor.matmul(out=hb[:], lhsT=aT_sb[q][:, i, s, :], rhs=vr_sb[:, s, :], start=True, stop=not is_x(r))
                 if is_x(r):
+                    nc.tensor.matmul(out=hb[:], lhsT=aT_sb[q][:, i, s, :], rhs=vr_sb[:, s, :], start=True, stop=False)
                     nc.tensor.matmul(out=hb[:], lhsT=neg_i[:], rhs=h_sb[q][:, i, c], start=False, stop=True)
+                else:
+                    nc.tensor.matmul(out=hb[:], lhsT=aT_sb[q][:, i, s, :], rhs=vrp_sb[:, s, :], start=True, stop=False)
+                    for je in range(4):
+                        nc.tensor.matmul(
+                            out=hb[:, P * je : P * je + P],
+                            lhsT=nh_sb[r][:, 2 * s + je // 2, je % 2, :],
+                            rhs=ident_f[:],
+                            start=False,
+                            stop=(je == 3),
+                            is_transpose=True,
+                        )
                 hh_ps[r].append(hb)
             o_sb[r] = work.tile([P, D], F32, name="o_t", tag="o", bufs=8)
-
-        def p3(r):
-            q, i = divmod(r, ROWS)
-            for s in range(S):
-                c = slice(DS * s, DS * s + DS)
-                nc.vector.tensor_tensor(out=o_sb[r][:, c], in0=hh_ps[r][s][:], in1=h_sb[q][:, i, c], op=ALU.subtract)
 
         def p1(r):
             for u in range(2):
@@ -175,12 +205,24 @@ def tile_tpru_pb_t_kernel(tc, a, vr, h, x2g, w_g, b_g, bg, out):
         def p4x(r):
             for s in range(S):
                 c = slice(DS * s, DS * s + DS)
-                nc.vector.tensor_tensor(out=o_sb[r][:, c], in0=hh_ps[r][s][:], in1=z_sb[r][:, c], op=ALU.mult)
+                if is_x(r):
+                    nc.vector.tensor_tensor(out=o_sb[r][:, c], in0=hh_ps[r][s][:], in1=z_sb[r][:, c], op=ALU.mult)
+                else:
+                    nc.vector.tensor_tensor(
+                        out=o_sb[r][:, c].rearrange("r (j p e) -> r j p e", j=2, p=P, e=2),
+                        in0=hh_ps[r][s][:].rearrange("r (j e p) -> r j p e", j=2, p=P, e=2),
+                        in1=z_sb[r][:, c].rearrange("r (j p e) -> r j p e", j=2, p=P, e=2),
+                        op=ALU.mult,
+                    )
 
         def finish(r):
             q, i = divmod(r, ROWS)
-            if not is_x(r):
-                nc.gpsimd.tensor_tensor(out=o_sb[r][:], in0=o_sb[r][:], in1=z_sb[r][:], op=ALU.mult)
+            if r == NT - 1:
+                for s in range(S):
+                    c = slice(DS * s, DS * s + DS)
+                    nc.vector.tensor_tensor(out=o_sb[r][:, c], in0=o_sb[r][:, c], in1=h_sb[q][:, i, c], op=ALU.add)
+                    nc.sync.dma_start(out=o_v[q][:, i, c], in_=o_sb[r][:, c])
+                return
             nc.gpsimd.tensor_tensor(out=o_sb[r][:], in0=o_sb[r][:], in1=h_sb[q][:, i, :], op=ALU.add)
             nc.sync.dma_start(out=o_v[q][:, i, :], in_=o_sb[r][:])
 
@@ -199,10 +241,7 @@ def tile_tpru_pb_t_kernel(tc, a, vr, h, x2g, w_g, b_g, bg, out):
                 nc.tensor.transpose(tpw[:, blk, :], wj[:, P * blk : P * blk + P], ident_f[:])
             src = tpw[:].rearrange("p (g u) r -> p g r u", g=2, u=2)
             dst = wg_f[:, :, P * j : P * j + P, :]
-            if j % 2 == 0:
-                nc.scalar.copy(out=dst, in_=src)
-            else:
-                nc.vector.tensor_copy(out=dst, in_=src)
+            nc.scalar.copy(out=dst, in_=src)
             if j == 3:
                 front(0)
             if j % 4 == 3:
@@ -218,8 +257,6 @@ def tile_tpru_pb_t_kernel(tc, a, vr, h, x2g, w_g, b_g, bg, out):
         front(1)
         mm(0)
         hh(0)
-        if not is_x(0):
-            p3(0)
 
         for r in range(NT):
             q, i = divmod(r, ROWS)
@@ -236,10 +273,7 @@ def tile_tpru_pb_t_kernel(tc, a, vr, h, x2g, w_g, b_g, bg, out):
                 mm(r + 1)
             if r + 1 + P0_AHEAD < NT:
                 p0(r + 1 + P0_AHEAD)
-            if is_x(r):
-                p4x(r)
+            p4x(r)
             if r + 1 < NT:
                 hh(r + 1)
-                if not is_x(r + 1):
-                    p3(r + 1)
             finish(r)

@@ -18,6 +18,7 @@ ROWS = 4
 GROUPS = B // (P * ROWS)
 NT = GROUPS * ROWS
 P0_AHEAD = 5
+FRONT_AHEAD = 5
 
 FLOPS = 2 * B * D * D + 2 * B * N * D
 
@@ -46,7 +47,7 @@ def tile_tpru_pb_t_kernel(tc, a, vr, h, x2g, w_g, b_g, bg, out):
         psb = ctx.enter_context(tc.psum_pool(name="psb", bufs=1))
 
         h_sb, x_sb, a_sb, aT_sb = {}, {}, {}, {}
-        hc_sb, hs_sb, acc_ps, hh_ps, z_sb, o_sb, nh_sb = {}, {}, {}, {}, {}, {}, {}
+        hc_sb, hs_sb, acc_ps, hh_ps, z_sb, o_sb, nh_sb, hg_sb = {}, {}, {}, {}, {}, {}, {}, {}
 
         def load_x(q):
             x_sb[q] = ld.tile([P, ROWS, D], BF16, name="x_t", tag="x")
@@ -132,31 +133,38 @@ def tile_tpru_pb_t_kernel(tc, a, vr, h, x2g, w_g, b_g, bg, out):
 
         def front(r):
             q, i = divmod(r, ROWS)
+            if i == 0:
+                hg_sb[q] = work.tile([P, ROWS, D], BF16, name="hg", tag="hg", bufs=2, align_bytes=64)
+                hc_sb[q] = work.tile([P, ROWS, 2, P], U32, name="hc", tag="hc", bufs=2, align_bytes=64)
+                hs_sb[q] = work.tile([P, ROWS, 2, P], U8, name="hs", tag="hs", bufs=2, align_bytes=64)
             tph = psum.tile([P, 4, P], F32, name="tph", tag="tp")
             hw = h_sb[q][:, i, :].bitcast(F32)
             for blk in range(4):
                 nc.tensor.transpose(tph[:, blk, :], hw[:, P * blk : P * blk + P], ident_f[:])
-            hg = work.tile([P, D], BF16, name="hg", tag="hg", align_bytes=64)
             nc.scalar.copy(
-                out=hg[:].bitcast(F32).rearrange("p (g r u) -> p g r u", g=2, r=P, u=2),
+                out=hg_sb[q][:, i, :].bitcast(F32).rearrange("p (g r u) -> p g r u", g=2, r=P, u=2),
                 in_=tph[:].rearrange("p (g u) r -> p g r u", g=2, u=2),
             )
-            if not is_x(r):
-                nh_sb[r] = work.tile([P, 4, 2, P], F32, name="nh", tag="nh", bufs=3)
-                nc.scalar.mul(
-                    out=nh_sb[r][:],
-                    in_=tph[:].rearrange("p j r -> p (j r)").bitcast(BF16).rearrange("p (j r e) -> p j e r", j=4, r=P, e=2),
-                    mul=-1.0,
-                )
-            hc_sb[r] = work.tile([P, 2, P], U32, name="hc", tag="hc", align_bytes=64)
-            hs_sb[r] = work.tile([P, 2, P], U8, name="hs", tag="hs", align_bytes=64)
+
+        def quant(q, i0, n):
             nc.vector.quantize_mx(
-                out=hc_sb[r][:].rearrange("p g r -> p (g r)").bitcast(FP8X4),
-                scales=hs_sb[r][:].rearrange("p g r -> p (g r)"),
-                in_=hg[:],
+                out=hc_sb[q][:, i0 : i0 + n, :, :].rearrange("p i g r -> p (i g r)").bitcast(FP8X4),
+                scales=hs_sb[q][:, i0 : i0 + n, :, :].rearrange("p i g r -> p (i g r)"),
+                in_=hg_sb[q][:, i0 : i0 + n, :].rearrange("p i x -> p (i x)"),
             )
 
+        def nh_make(r):
+            q, i = divmod(r, ROWS)
+            nh_sb[r] = work.tile([P, 2, 4, P], F32, name="nh", tag="nh", bufs=3)
+            for g in range(2):
+                nc.scalar.mul(
+                    out=nh_sb[r][:, g, :, :],
+                    in_=hg_sb[q][:, i, 4 * P * g : 4 * P * g + 4 * P].rearrange("p (r t) -> p t r", r=P, t=4),
+                    mul=-1.0,
+                )
+
         def mm(r):
+            q, i = divmod(r, ROWS)
             acc_ps[r] = []
             for u in range(2):
                 c = slice(DS * u, DS * u + DS)
@@ -164,8 +172,8 @@ def tile_tpru_pb_t_kernel(tc, a, vr, h, x2g, w_g, b_g, bg, out):
                 for g in range(2):
                     nc.tensor.matmul_mx(
                         out=acc[:],
-                        lhsT=hc_sb[r][:, g, :].bitcast(FP8X4),
-                        lhsT_scale=hs_sb[r][:, g, :],
+                        lhsT=hc_sb[q][:, i, g, :].bitcast(FP8X4),
+                        lhsT_scale=hs_sb[q][:, i, g, :],
                         rhs=wc[:, g, c].bitcast(FP8X4),
                         rhs_scale=ws[:, g, c],
                         start=(g == 0),
@@ -187,14 +195,14 @@ def tile_tpru_pb_t_kernel(tc, a, vr, h, x2g, w_g, b_g, bg, out):
                     for je in range(4):
                         nc.tensor.matmul(
                             out=hb[:, P * je : P * je + P],
-                            lhsT=nh_sb[r][:, 2 * s + je // 2, je % 2, :],
+                            lhsT=nh_sb[r][:, s, je, :],
                             rhs=ident_f[:],
                             start=False,
                             stop=(je == 3),
                             is_transpose=True,
                         )
                 hh_ps[r].append(hb)
-            o_sb[r] = work.tile([P, D], F32, name="o_t", tag="o", bufs=8)
+            o_sb[r] = work.tile([P, D], F32, name="o_t", tag="o", bufs=6)
 
         def p1(r):
             for u in range(2):
@@ -244,6 +252,7 @@ def tile_tpru_pb_t_kernel(tc, a, vr, h, x2g, w_g, b_g, bg, out):
             nc.scalar.copy(out=dst, in_=src)
             if j == 3:
                 front(0)
+                quant(0, 0, 1)
             if j % 4 == 3:
                 u = j // 4
                 for g in range(2):
@@ -254,7 +263,11 @@ def tile_tpru_pb_t_kernel(tc, a, vr, h, x2g, w_g, b_g, bg, out):
                     )
 
         aprep(0)
-        front(1)
+        for r in range(1, FRONT_AHEAD):
+            front(r)
+            if r < ROWS:
+                quant(0, r, 1)
+        nh_make(1)
         mm(0)
         hh(0)
 
@@ -266,8 +279,13 @@ def tile_tpru_pb_t_kernel(tc, a, vr, h, x2g, w_g, b_g, bg, out):
                 load_a(q + 2)
             if i == 2 and q + 1 < GROUPS:
                 aprep(q + 1)
-            if r + 2 < NT:
-                front(r + 2)
+            rf = r + FRONT_AHEAD
+            if rf < NT:
+                front(rf)
+                if rf % ROWS == ROWS - 1:
+                    quant(rf // ROWS, 0, ROWS)
+            if r + 2 < NT and not is_x(r + 2):
+                nh_make(r + 2)
             p1(r)
             if r + 1 < NT:
                 mm(r + 1)

@@ -17,8 +17,8 @@ DS = D // S
 ROWS = 4
 GROUPS = B // (P * ROWS)
 NT = GROUPS * ROWS
-P0_AHEAD = 5
-FRONT_AHEAD = 5
+K0 = 6
+TF = 5
 
 FLOPS = 2 * B * D * D + 2 * B * N * D
 
@@ -28,7 +28,7 @@ def is_x(r):
 
 
 def p0_on_gpsimd(r):
-    return r % 3 == 0
+    return r >= 6 and r % 3 == 0
 
 
 def tile_tpru_pb_t_kernel(tc, a, vr, h, x2g, w_g, b_g, bg, out):
@@ -42,12 +42,12 @@ def tile_tpru_pb_t_kernel(tc, a, vr, h, x2g, w_g, b_g, bg, out):
     with ExitStack() as ctx:
         const = ctx.enter_context(tc.tile_pool(name="const", bufs=1))
         ld = ctx.enter_context(tc.tile_pool(name="ld", bufs=3))
-        work = ctx.enter_context(tc.tile_pool(name="work", bufs=3))
+        work = ctx.enter_context(tc.tile_pool(name="work", bufs=2))
         psum = ctx.enter_context(tc.psum_pool(name="psum", bufs=2))
         psb = ctx.enter_context(tc.psum_pool(name="psb", bufs=1))
 
-        h_sb, x_sb, a_sb, aT_sb = {}, {}, {}, {}
-        hc_sb, hs_sb, acc_ps, hh_ps, z_sb, o_sb, nh_sb, hg_sb = {}, {}, {}, {}, {}, {}, {}, {}
+        h_sb, x_sb, a_sb, aT_sb, tp_ps, ta_ps = {}, {}, {}, {}, {}, {}
+        hg_sb, hc_sb, hs_sb, nh_sb, acc_ps, hh_ps, z_sb, o_sb = {}, {}, {}, {}, {}, {}, {}, {}
 
         def load_x(q):
             x_sb[q] = ld.tile([P, ROWS, D], BF16, name="x_t", tag="x")
@@ -74,88 +74,100 @@ def tile_tpru_pb_t_kernel(tc, a, vr, h, x2g, w_g, b_g, bg, out):
         bg_b = const.tile([P, 1], BF16, name="bg_b")
         nc.sync.dma_start(out=bg_b[:], in_=bg.partition_broadcast(P))
 
-        load_x(0)
-        wraw = const.tile([P, 8, D], BF16, name="wraw")
-        nc.sync.dma_start(out=wraw[:, 0:4, :], in_=w_v[:, 0:4, :])
-        h_sb[0] = ld.tile([P, ROWS, D], BF16, name="h_t", tag="h", bufs=4)
-        nc.sync.dma_start(out=h_sb[0][:, 0:1, :], in_=h_v[0][:, 0:1, :])
-        nc.sync.dma_start(out=wraw[:, 4:8, :], in_=w_v[:, 4:8, :])
-        load_a(0)
+        wc = const.tile([P, 2, D], U32, name="wc", align_bytes=64)
+        ws = const.tile([P, 2, D], U8, name="ws", align_bytes=64)
         vr_sb = const.tile([P, S, DS], BF16, name="vr_sb")
-        nc.sync.dma_start(out=vr_sb[:], in_=vr)
-        nc.sync.dma_start(out=h_sb[0][:, 1:4, :], in_=h_v[0][:, 1:4, :])
         vrp_sb = const.tile([P, S, DS], BF16, name="vrp_sb")
-        nc.vector.tensor_copy(
-            out=vrp_sb[:].rearrange("n s (j e p) -> n (s j) e p", j=2, e=2, p=P),
-            in_=vr_sb[:].rearrange("n s (j p e) -> n (s j) e p", j=2, e=2, p=P),
-        )
-        load_x(1)
-        load_h(1)
-        load_a(1)
-
-        b_t = psum.tile([P, P], BF16, name="b_t", tag="tp")
-        nc.tensor.transpose(b_t[:], brow[:], ident_b[:])
-        bg_f = const.tile([P, 1], F32, name="bg_f")
-        nc.vector.tensor_copy(out=bg_f[:], in_=bg_b[:])
-        bcol = const.tile([P, 8], F32, name="bcol")
-        nc.vector.tensor_scalar_add(out=bcol[:], in0=b_t[:, 0:8], scalar1=bg_f[:, 0:1])
-        brep = const.tile([P, 8, P], F32, name="brep")
-        nc.vector.tensor_copy(out=brep[:], in_=bcol[:].unsqueeze(2).to_broadcast([P, 8, P]))
-        bias_ps = []
-        for u in range(2):
-            bias_ps.append(psb.tile([P, DS], F32, name="bias%d" % u))
-        for j in range(8):
-            nc.tensor.transpose(bias_ps[j // 4][:, P * (j % 4) : P * (j % 4) + P], brep[:, j, :], ident_f[:])
-
         bias_sb = const.tile([P, D], F32, name="bias_sb")
-        for u in range(2):
-            nc.scalar.copy(out=bias_sb[:, DS * u : DS * u + DS], in_=bias_ps[u][:])
 
-        def p0(r):
-            q, i = divmod(r, ROWS)
-            z_sb[r] = work.tile([P, D], F32, name="z_t", tag="z", bufs=8)
-            if p0_on_gpsimd(r):
-                nc.gpsimd.tensor_tensor(out=z_sb[r][:], in0=x_sb[q][:, i, :], in1=bias_sb[:], op=ALU.add)
-                return
-            for u in range(2):
-                c = slice(DS * u, DS * u + DS)
-                nc.vector.tensor_tensor(out=z_sb[r][:, c], in0=bias_ps[u][:], in1=x_sb[q][:, i, c], op=ALU.add)
+        wtmp = tc.tile_pool(name="wtmp", bufs=1)
+        with wtmp as wt:
+            load_x(0)
+            wraw = wt.tile([P, 8, D], BF16, name="wraw")
+            nc.sync.dma_start(out=wraw[:, 0:4, :], in_=w_v[:, 0:4, :])
+            h_sb[0] = ld.tile([P, ROWS, D], BF16, name="h_t", tag="h", bufs=4)
+            nc.sync.dma_start(out=h_sb[0][:, 0:1, :], in_=h_v[0][:, 0:1, :])
+            nc.sync.dma_start(out=wraw[:, 4:8, :], in_=w_v[:, 4:8, :])
+            load_a(0)
+            nc.sync.dma_start(out=vr_sb[:], in_=vr)
+            nc.sync.dma_start(out=h_sb[0][:, 1:4, :], in_=h_v[0][:, 1:4, :])
+            load_x(1)
+            load_h(1)
+            load_a(1)
 
-        def aprep(q):
-            tpa = psum.tile([P, ROWS, P], F32, name="tpa", tag="tp")
-            for i in range(ROWS):
-                nc.tensor.transpose(tpa[:, i, :], a_sb[q][:, i, :].bitcast(F32), ident_f[:])
-            aT_sb[q] = work.tile([P, ROWS, S, P], BF16, name="aT", tag="aT", bufs=2)
-            nc.scalar.copy(
-                out=aT_sb[q][:],
-                in_=tpa[:].rearrange("p i b -> p (i b)").bitcast(BF16).rearrange("p (i b s) -> p i s b", i=ROWS, b=P, s=S),
+            nc.vector.tensor_copy(
+                out=vrp_sb[:].rearrange("n s (j e p) -> n (s j) e p", j=2, e=2, p=P),
+                in_=vr_sb[:].rearrange("n s (j p e) -> n (s j) e p", j=2, e=2, p=P),
             )
 
-        def front(r):
+            b_t = psum.tile([P, P], BF16, name="b_t", tag="tp")
+            nc.tensor.transpose(b_t[:], brow[:], ident_b[:])
+            bg_f = const.tile([P, 1], F32, name="bg_f")
+            nc.vector.tensor_copy(out=bg_f[:], in_=bg_b[:])
+            bcol = const.tile([P, 8], F32, name="bcol")
+            nc.vector.tensor_scalar_add(out=bcol[:], in0=b_t[:, 0:8], scalar1=bg_f[:, 0:1])
+            brep = wt.tile([P, 8, P], F32, name="brep")
+            nc.vector.tensor_copy(out=brep[:], in_=bcol[:].unsqueeze(2).to_broadcast([P, 8, P]))
+            bias_ps = []
+            for u in range(2):
+                bias_ps.append(psb.tile([P, DS], F32, name="bias%d" % u))
+            for j in range(8):
+                nc.tensor.transpose(bias_ps[j // 4][:, P * (j % 4) : P * (j % 4) + P], brep[:, j, :], ident_f[:])
+            for u in range(2):
+                nc.scalar.copy(out=bias_sb[:, DS * u : DS * u + DS], in_=bias_ps[u][:])
+
+            wg = wt.tile([P, 2 * D * 4], BF16, name="wg", align_bytes=64)
+            wg_f = wg[:].bitcast(F32).rearrange("p (g c u) -> p g c u", g=2, c=D, u=2)
+            wg_q = wg[:].rearrange("p (g x) -> p g x", g=2)
+            for j in range(8):
+                tpw = psum.tile([P, 4, P], F32, name="tpw", tag="tp")
+                wj = wraw[:, j, :].bitcast(F32)
+                for blk in range(4):
+                    nc.tensor.transpose(tpw[:, blk, :], wj[:, P * blk : P * blk + P], ident_f[:])
+                nc.scalar.copy(
+                    out=wg_f[:, :, P * j : P * j + P, :],
+                    in_=tpw[:].rearrange("p (g u) r -> p g r u", g=2, u=2),
+                )
+                if j % 4 == 3:
+                    u = j // 4
+                    for g in range(2):
+                        nc.vector.quantize_mx(
+                            out=wc[:, g, DS * u : DS * u + DS].bitcast(FP8X4),
+                            scales=ws[:, g, DS * u : DS * u + DS],
+                            in_=wg_q[:, g, 4 * DS * u : 4 * DS * u + 4 * DS],
+                        )
+
+        late = ctx.enter_context(tc.tile_pool(name="late", bufs=3))
+
+        def t_h(r):
             q, i = divmod(r, ROWS)
-            if i == 0:
-                hg_sb[q] = work.tile([P, ROWS, D], BF16, name="hg", tag="hg", bufs=2, align_bytes=64)
-                hc_sb[q] = work.tile([P, ROWS, 2, P], U32, name="hc", tag="hc", bufs=2, align_bytes=64)
-                hs_sb[q] = work.tile([P, ROWS, 2, P], U8, name="hs", tag="hs", bufs=2, align_bytes=64)
-            tph = psum.tile([P, 4, P], F32, name="tph", tag="tp")
+            tp_ps[r] = psum.tile([P, 4, P], F32, name="tph", tag="tp")
             hw = h_sb[q][:, i, :].bitcast(F32)
             for blk in range(4):
-                nc.tensor.transpose(tph[:, blk, :], hw[:, P * blk : P * blk + P], ident_f[:])
+                nc.tensor.transpose(tp_ps[r][:, blk, :], hw[:, P * blk : P * blk + P], ident_f[:])
+
+        def c_h(r):
+            q, i = divmod(r, ROWS)
+            if i == 0:
+                hg_sb[q] = work.tile([P, ROWS, D], BF16, name="hg", tag="hg", align_bytes=64)
+                hc_sb[q] = work.tile([P, ROWS, 2, P], U32, name="hc", tag="hc", align_bytes=64)
+                hs_sb[q] = work.tile([P, ROWS, 2, P], U8, name="hs", tag="hs", align_bytes=64)
             nc.scalar.copy(
                 out=hg_sb[q][:, i, :].bitcast(F32).rearrange("p (g r u) -> p g r u", g=2, r=P, u=2),
-                in_=tph[:].rearrange("p (g u) r -> p g r u", g=2, u=2),
+                in_=tp_ps[r][:].rearrange("p (g u) r -> p g r u", g=2, u=2),
             )
 
-        def quant(q, i0, n):
+        def quant(r0):
+            q, i0 = divmod(r0, ROWS)
             nc.vector.quantize_mx(
-                out=hc_sb[q][:, i0 : i0 + n, :, :].rearrange("p i g r -> p (i g r)").bitcast(FP8X4),
-                scales=hs_sb[q][:, i0 : i0 + n, :, :].rearrange("p i g r -> p (i g r)"),
-                in_=hg_sb[q][:, i0 : i0 + n, :].rearrange("p i x -> p (i x)"),
+                out=hc_sb[q][:, i0 : i0 + 2, :, :].rearrange("p i g r -> p (i g r)").bitcast(FP8X4),
+                scales=hs_sb[q][:, i0 : i0 + 2, :, :].rearrange("p i g r -> p (i g r)"),
+                in_=hg_sb[q][:, i0 : i0 + 2, :].rearrange("p i x -> p (i x)"),
             )
 
         def nh_make(r):
             q, i = divmod(r, ROWS)
-            nh_sb[r] = work.tile([P, 2, 4, P], F32, name="nh", tag="nh", bufs=3)
+            nh_sb[r] = late.tile([P, 2, 4, P], F32, name="nh", tag="nh")
             for g in range(2):
                 nc.scalar.mul(
                     out=nh_sb[r][:, g, :, :],
@@ -163,135 +175,136 @@ def tile_tpru_pb_t_kernel(tc, a, vr, h, x2g, w_g, b_g, bg, out):
                     mul=-1.0,
                 )
 
-        def mm(r):
+        def t_a(q):
+            ta_ps[q] = psum.tile([P, ROWS, P], F32, name="tpa", tag="tp")
+            for i in range(ROWS):
+                nc.tensor.transpose(ta_ps[q][:, i, :], a_sb[q][:, i, :].bitcast(F32), ident_f[:])
+
+        def c_a(q):
+            aT_sb[q] = work.tile([P, ROWS, S, P], BF16, name="aT", tag="aT")
+            nc.scalar.copy(
+                out=aT_sb[q][:],
+                in_=ta_ps[q][:].rearrange("p i b -> p (i b)").bitcast(BF16).rearrange("p (i b s) -> p i s b", i=ROWS, b=P, s=S),
+            )
+
+        def p0(r):
             q, i = divmod(r, ROWS)
-            acc_ps[r] = []
-            for u in range(2):
-                c = slice(DS * u, DS * u + DS)
-                acc = psum.tile([P, DS], F32, name="acc", tag="h2g")
-                for g in range(2):
-                    nc.tensor.matmul_mx(
-                        out=acc[:],
-                        lhsT=hc_sb[q][:, i, g, :].bitcast(FP8X4),
-                        lhsT_scale=hs_sb[q][:, i, g, :],
-                        rhs=wc[:, g, c].bitcast(FP8X4),
-                        rhs_scale=ws[:, g, c],
-                        start=(g == 0),
-                        stop=(g == 1),
-                    )
-                acc_ps[r].append(acc)
-
-        def hh(r):
-            q, i = divmod(r, ROWS)
-            hh_ps[r] = []
-            for s in range(S):
-                c = slice(DS * s, DS * s + DS)
-                hb = psum.tile([P, DS], F32, name="hb", tag="hh")
-                if is_x(r):
-                    nc.tensor.matmul(out=hb[:], lhsT=aT_sb[q][:, i, s, :], rhs=vr_sb[:, s, :], start=True, stop=False)
-                    nc.tensor.matmul(out=hb[:], lhsT=neg_i[:], rhs=h_sb[q][:, i, c], start=False, stop=True)
-                else:
-                    nc.tensor.matmul(out=hb[:], lhsT=aT_sb[q][:, i, s, :], rhs=vrp_sb[:, s, :], start=True, stop=False)
-                    for je in range(4):
-                        nc.tensor.matmul(
-                            out=hb[:, P * je : P * je + P],
-                            lhsT=nh_sb[r][:, s, je, :],
-                            rhs=ident_f[:],
-                            start=False,
-                            stop=(je == 3),
-                            is_transpose=True,
-                        )
-                hh_ps[r].append(hb)
-            o_sb[r] = work.tile([P, D], F32, name="o_t", tag="o", bufs=6)
-
-        def p1(r):
-            for u in range(2):
-                c = slice(DS * u, DS * u + DS)
-                nc.vector.tensor_tensor(out=z_sb[r][:, c], in0=acc_ps[r][u][:], in1=z_sb[r][:, c], op=ALU.add)
-            nc.scalar.activation(out=z_sb[r][:], in_=z_sb[r][:], func=ACT.Sigmoid)
-
-        def p4x(r):
-            for s in range(S):
-                c = slice(DS * s, DS * s + DS)
-                if is_x(r):
-                    nc.vector.tensor_tensor(out=o_sb[r][:, c], in0=hh_ps[r][s][:], in1=z_sb[r][:, c], op=ALU.mult)
-                else:
-                    nc.vector.tensor_tensor(
-                        out=o_sb[r][:, c].rearrange("r (j p e) -> r j p e", j=2, p=P, e=2),
-                        in0=hh_ps[r][s][:].rearrange("r (j e p) -> r j p e", j=2, p=P, e=2),
-                        in1=z_sb[r][:, c].rearrange("r (j p e) -> r j p e", j=2, p=P, e=2),
-                        op=ALU.mult,
-                    )
-
-        def finish(r):
-            q, i = divmod(r, ROWS)
-            if r == NT - 1:
-                for s in range(S):
-                    c = slice(DS * s, DS * s + DS)
-                    nc.vector.tensor_tensor(out=o_sb[r][:, c], in0=o_sb[r][:, c], in1=h_sb[q][:, i, c], op=ALU.add)
-                    nc.sync.dma_start(out=o_v[q][:, i, c], in_=o_sb[r][:, c])
+            z_sb[r] = work.tile([P, D], F32, name="z_t", tag="z", bufs=K0 + 3)
+            if p0_on_gpsimd(r):
+                nc.gpsimd.tensor_tensor(out=z_sb[r][:], in0=x_sb[q][:, i, :], in1=bias_sb[:], op=ALU.add)
                 return
-            nc.gpsimd.tensor_tensor(out=o_sb[r][:], in0=o_sb[r][:], in1=h_sb[q][:, i, :], op=ALU.add)
+            for u in range(2):
+                c = slice(DS * u, DS * u + DS)
+                nc.vector.tensor_tensor(out=z_sb[r][:, c], in0=bias_ps[u][:], in1=x_sb[q][:, i, c], op=ALU.add)
+
+        def mm(r, u):
+            q, i = divmod(r, ROWS)
+            c = slice(DS * u, DS * u + DS)
+            acc = psum.tile([P, DS], F32, name="acc", tag="h2g")
+            for g in range(2):
+                nc.tensor.matmul_mx(
+                    out=acc[:],
+                    lhsT=hc_sb[q][:, i, g, :].bitcast(FP8X4),
+                    lhsT_scale=hs_sb[q][:, i, g, :],
+                    rhs=wc[:, g, c].bitcast(FP8X4),
+                    rhs_scale=ws[:, g, c],
+                    start=(g == 0),
+                    stop=(g == 1),
+                )
+            acc_ps[(r, u)] = acc
+
+        def p1(r, u):
+            c = slice(DS * u, DS * u + DS)
+            nc.vector.tensor_tensor(out=z_sb[r][:, c], in0=acc_ps[(r, u)][:], in1=z_sb[r][:, c], op=ALU.add)
+
+        def d_open(r, s):
+            q, i = divmod(r, ROWS)
+            hb = psum.tile([P, DS], F32, name="hb", tag="hh")
+            rhs = vr_sb if is_x(r) else vrp_sb
+            nc.tensor.matmul(out=hb[:], lhsT=aT_sb[q][:, i, s, :], rhs=rhs[:, s, :], start=True, stop=False)
+            hh_ps[(r, s)] = hb
+
+        def d_close(r, s):
+            q, i = divmod(r, ROWS)
+            hb = hh_ps[(r, s)]
+            if is_x(r):
+                nc.tensor.matmul(out=hb[:], lhsT=neg_i[:], rhs=h_sb[q][:, i, DS * s : DS * s + DS], start=False, stop=True)
+                return
+            for t in range(4):
+                nc.tensor.matmul(
+                    out=hb[:, P * t : P * t + P],
+                    lhsT=nh_sb[r][:, s, t, :],
+                    rhs=ident_f[:],
+                    start=False,
+                    stop=(t == 3),
+                    is_transpose=True,
+                )
+
+        def p4(r, s):
+            c = slice(DS * s, DS * s + DS)
+            if s == 0:
+                o_sb[r] = late.tile([P, D], F32, name="o_t", tag="o", bufs=6)
+            if is_x(r):
+                nc.vector.tensor_tensor(out=o_sb[r][:, c], in0=hh_ps[(r, s)][:], in1=z_sb[r][:, c], op=ALU.mult)
+            else:
+                nc.vector.tensor_tensor(
+                    out=o_sb[r][:, c].rearrange("r (j p e) -> r j p e", j=2, p=P, e=2),
+                    in0=hh_ps[(r, s)][:].rearrange("r (j e p) -> r j p e", j=2, p=P, e=2),
+                    in1=z_sb[r][:, c].rearrange("r (j p e) -> r j p e", j=2, p=P, e=2),
+                    op=ALU.mult,
+                )
+
+        def store(r):
+            q, i = divmod(r, ROWS)
             nc.sync.dma_start(out=o_v[q][:, i, :], in_=o_sb[r][:])
 
-        for r in range(P0_AHEAD + 1):
-            p0(r)
+        def ok(r):
+            return 0 <= r < NT
 
-        wg = const.tile([P, 2 * D * 4], BF16, name="wg", align_bytes=64)
-        wg_f = wg[:].bitcast(F32).rearrange("p (g c u) -> p g c u", g=2, c=D, u=2)
-        wg_q = wg[:].rearrange("p (g x) -> p g x", g=2)
-        wc = const.tile([P, 2, D], U32, name="wc", align_bytes=64)
-        ws = const.tile([P, 2, D], U8, name="ws", align_bytes=64)
-        for j in range(8):
-            tpw = psum.tile([P, 4, P], F32, name="tpw", tag="tp")
-            wj = wraw[:, j, :].bitcast(F32)
-            for blk in range(4):
-                nc.tensor.transpose(tpw[:, blk, :], wj[:, P * blk : P * blk + P], ident_f[:])
-            src = tpw[:].rearrange("p (g u) r -> p g r u", g=2, u=2)
-            dst = wg_f[:, :, P * j : P * j + P, :]
-            nc.scalar.copy(out=dst, in_=src)
-            if j == 3:
-                front(0)
-                quant(0, 0, 1)
-            if j % 4 == 3:
-                u = j // 4
-                for g in range(2):
-                    nc.vector.quantize_mx(
-                        out=wc[:, g, DS * u : DS * u + DS].bitcast(FP8X4),
-                        scales=ws[:, g, DS * u : DS * u + DS],
-                        in_=wg_q[:, g, 4 * DS * u : 4 * DS * u + 4 * DS],
-                    )
-
-        aprep(0)
-        for r in range(1, FRONT_AHEAD):
-            front(r)
-            if r < ROWS:
-                quant(0, r, 1)
-        nh_make(1)
-        mm(0)
-        hh(0)
-
-        for r in range(NT):
-            q, i = divmod(r, ROWS)
-            if i == 0 and q + 2 < GROUPS:
-                load_x(q + 2)
-                load_h(q + 2)
-                load_a(q + 2)
-            if i == 2 and q + 1 < GROUPS:
-                aprep(q + 1)
-            rf = r + FRONT_AHEAD
-            if rf < NT:
-                front(rf)
-                if rf % ROWS == ROWS - 1:
-                    quant(rf // ROWS, 0, ROWS)
-            if r + 2 < NT and not is_x(r + 2):
-                nh_make(r + 2)
-            p1(r)
-            if r + 1 < NT:
-                mm(r + 1)
-            if r + 1 + P0_AHEAD < NT:
-                p0(r + 1 + P0_AHEAD)
-            p4x(r)
-            if r + 1 < NT:
-                hh(r + 1)
-            finish(r)
+        with tc.manual_schedule():
+            for r in range(-K0, NT + 3):
+                if r >= -ROWS and r % ROWS == 0 and r // ROWS + 3 < GROUPS:
+                    load_x(r // ROWS + 3)
+                if r >= -1 and r % ROWS == ROWS - 1 and (r + 9) // ROWS < GROUPS:
+                    load_h((r + 9) // ROWS)
+                    load_a((r + 9) // ROWS)
+                for u in range(2):
+                    if ok(r):
+                        p1(r, u)
+                    if ok(r + 1):
+                        mm(r + 1, u)
+                if ok(r):
+                    nc.scalar.activation(out=z_sb[r][:], in_=z_sb[r][:], func=ACT.Sigmoid)
+                if ok(r + 4):
+                    c_h(r + 4)
+                if ok(r - 1):
+                    for s in range(S):
+                        p4(r - 1, s)
+                        if r - 1 == NT - 1:
+                            c = slice(DS * s, DS * s + DS)
+                            nc.vector.tensor_tensor(
+                                out=o_sb[r - 1][:, c], in0=o_sb[r - 1][:, c], in1=h_sb[GROUPS - 1][:, ROWS - 1, c], op=ALU.add
+                            )
+                            nc.sync.dma_start(out=o_v[GROUPS - 1][:, ROWS - 1, c], in_=o_sb[r - 1][:, c])
+                if ok(r):
+                    for s in range(S):
+                        d_open(r, s)
+                    for s in range(S):
+                        d_close(r, s)
+                if (r + 2) % ROWS == 0 and ok(r + 2):
+                    c_a((r + 2) // ROWS)
+                if ok(r + 2) and not is_x(r + 2):
+                    nh_make(r + 2)
+                if ok(r + K0):
+                    p0(r + K0)
+                if ok(r + 2) and (r + 2) % 2 == 0:
+                    quant(r + 2)
+                if ok(r - 1) and r - 1 < NT - 1:
+                    q1, i1 = divmod(r - 1, ROWS)
+                    nc.gpsimd.tensor_tensor(out=o_sb[r - 1][:], in0=o_sb[r - 1][:], in1=h_sb[q1][:, i1, :], op=ALU.add)
+                if ok(r + TF):
+                    t_h(r + TF)
+                if (r + 3) % ROWS == 0 and ok(r + 3):
+                    t_a((r + 3) // ROWS)
+                if ok(r - 2) and r - 2 < NT - 1:
+                    store(r - 2)

@@ -28,7 +28,7 @@ def is_x(r):
 
 
 def p0_on_gpsimd(r):
-    return r >= 6 and r % 3 == 0
+    return False
 
 
 def tile_tpru_pb_t_kernel(tc, a, vr, h, x2g, w_g, b_g, bg, out):

@@ -17,18 +17,14 @@ DS = D // S
 ROWS = 4
 GROUPS = B // (P * ROWS)
 NT = GROUPS * ROWS
-K0 = 6
+K0 = 4
 TF = 5
 
 FLOPS = 2 * B * D * D + 2 * B * N * D
 
 
 def is_x(r):
-    return r % 2 == 0
-
-
-def p0_on_gpsimd(r):
-    return False
+    return r % 2 == 1
 
 
 def tile_tpru_pb_t_kernel(tc, a, vr, h, x2g, w_g, b_g, bg, out):
@@ -47,7 +43,7 @@ def tile_tpru_pb_t_kernel(tc, a, vr, h, x2g, w_g, b_g, bg, out):
         psb = ctx.enter_context(tc.psum_pool(name="psb", bufs=1))
 
         h_sb, x_sb, a_sb, aT_sb, tp_ps, ta_ps = {}, {}, {}, {}, {}, {}
-        hg_sb, hc_sb, hs_sb, nh_sb, acc_ps, hh_ps, z_sb, o_sb = {}, {}, {}, {}, {}, {}, {}, {}
+        hg_sb, hc_sb, hs_sb, acc_ps, hh_ps, z_sb, o_sb = {}, {}, {}, {}, {}, {}, {}
 
         def load_x(q):
             x_sb[q] = ld.tile([P, ROWS, D], BF16, name="x_t", tag="x")
@@ -77,8 +73,6 @@ def tile_tpru_pb_t_kernel(tc, a, vr, h, x2g, w_g, b_g, bg, out):
         wc = const.tile([P, 2, D], U32, name="wc", align_bytes=64)
         ws = const.tile([P, 2, D], U8, name="ws", align_bytes=64)
         vr_sb = const.tile([P, S, DS], BF16, name="vr_sb")
-        vrp_sb = const.tile([P, S, DS], BF16, name="vrp_sb")
-        bias_sb = const.tile([P, D], F32, name="bias_sb")
 
         wtmp = tc.tile_pool(name="wtmp", bufs=1)
         with wtmp as wt:
@@ -95,11 +89,6 @@ def tile_tpru_pb_t_kernel(tc, a, vr, h, x2g, w_g, b_g, bg, out):
             load_h(1)
             load_a(1)
 
-            nc.vector.tensor_copy(
-                out=vrp_sb[:].rearrange("n s (j e p) -> n (s j) e p", j=2, e=2, p=P),
-                in_=vr_sb[:].rearrange("n s (j p e) -> n (s j) e p", j=2, e=2, p=P),
-            )
-
             b_t = psum.tile([P, P], BF16, name="b_t", tag="tp")
             nc.tensor.transpose(b_t[:], brow[:], ident_b[:])
             bg_f = const.tile([P, 1], F32, name="bg_f")
@@ -113,8 +102,6 @@ def tile_tpru_pb_t_kernel(tc, a, vr, h, x2g, w_g, b_g, bg, out):
                 bias_ps.append(psb.tile([P, DS], F32, name="bias%d" % u))
             for j in range(8):
                 nc.tensor.transpose(bias_ps[j // 4][:, P * (j % 4) : P * (j % 4) + P], brep[:, j, :], ident_f[:])
-            for u in range(2):
-                nc.scalar.copy(out=bias_sb[:, DS * u : DS * u + DS], in_=bias_ps[u][:])
 
             wg = wt.tile([P, 2 * D * 4], BF16, name="wg", align_bytes=64)
             wg_f = wg[:].bitcast(F32).rearrange("p (g c u) -> p g c u", g=2, c=D, u=2)
@@ -165,16 +152,6 @@ def tile_tpru_pb_t_kernel(tc, a, vr, h, x2g, w_g, b_g, bg, out):
                 in_=hg_sb[q][:, i0 : i0 + 2, :].rearrange("p i x -> p (i x)"),
             )
 
-        def nh_make(r):
-            q, i = divmod(r, ROWS)
-            nh_sb[r] = late.tile([P, 2, 4, P], F32, name="nh", tag="nh")
-            for g in range(2):
-                nc.scalar.mul(
-                    out=nh_sb[r][:, g, :, :],
-                    in_=hg_sb[q][:, i, 4 * P * g : 4 * P * g + 4 * P].rearrange("p (r t) -> p t r", r=P, t=4),
-                    mul=-1.0,
-                )
-
         def t_a(q):
             ta_ps[q] = psum.tile([P, ROWS, P], F32, name="tpa", tag="tp")
             for i in range(ROWS):
@@ -189,10 +166,7 @@ def tile_tpru_pb_t_kernel(tc, a, vr, h, x2g, w_g, b_g, bg, out):
 
         def p0(r):
             q, i = divmod(r, ROWS)
-            z_sb[r] = work.tile([P, D], F32, name="z_t", tag="z", bufs=K0 + 3)
-            if p0_on_gpsimd(r):
-                nc.gpsimd.tensor_tensor(out=z_sb[r][:], in0=x_sb[q][:, i, :], in1=bias_sb[:], op=ALU.add)
-                return
+            z_sb[r] = work.tile([P, D], F32, name="z_t", tag="z", bufs=K0 + 5)
             for u in range(2):
                 c = slice(DS * u, DS * u + DS)
                 nc.vector.tensor_tensor(out=z_sb[r][:, c], in0=bias_ps[u][:], in1=x_sb[q][:, i, c], op=ALU.add)
@@ -220,8 +194,7 @@ def tile_tpru_pb_t_kernel(tc, a, vr, h, x2g, w_g, b_g, bg, out):
         def d_open(r, s):
             q, i = divmod(r, ROWS)
             hb = psum.tile([P, DS], F32, name="hb", tag="hh")
-            rhs = vr_sb if is_x(r) else vrp_sb
-            nc.tensor.matmul(out=hb[:], lhsT=aT_sb[q][:, i, s, :], rhs=rhs[:, s, :], start=True, stop=False)
+            nc.tensor.matmul(out=hb[:], lhsT=aT_sb[q][:, i, s, :], rhs=vr_sb[:, s, :], start=True, stop=not is_x(r))
             hh_ps[(r, s)] = hb
 
         def d_close(r, s):
@@ -229,30 +202,16 @@ def tile_tpru_pb_t_kernel(tc, a, vr, h, x2g, w_g, b_g, bg, out):
             hb = hh_ps[(r, s)]
             if is_x(r):
                 nc.tensor.matmul(out=hb[:], lhsT=neg_i[:], rhs=h_sb[q][:, i, DS * s : DS * s + DS], start=False, stop=True)
-                return
-            for t in range(4):
-                nc.tensor.matmul(
-                    out=hb[:, P * t : P * t + P],
-                    lhsT=nh_sb[r][:, s, t, :],
-                    rhs=ident_f[:],
-                    start=False,
-                    stop=(t == 3),
-                    is_transpose=True,
-                )
 
         def p4(r, s):
             c = slice(DS * s, DS * s + DS)
             if s == 0:
-                o_sb[r] = late.tile([P, D], F32, name="o_t", tag="o", bufs=6)
+                o_sb[r] = late.tile([P, D], F32, name="o_t", tag="o", bufs=7)
             if is_x(r):
                 nc.vector.tensor_tensor(out=o_sb[r][:, c], in0=hh_ps[(r, s)][:], in1=z_sb[r][:, c], op=ALU.mult)
             else:
-                nc.vector.tensor_tensor(
-                    out=o_sb[r][:, c].rearrange("r (j p e) -> r j p e", j=2, p=P, e=2),
-                    in0=hh_ps[(r, s)][:].rearrange("r (j e p) -> r j p e", j=2, p=P, e=2),
-                    in1=z_sb[r][:, c].rearrange("r (j p e) -> r j p e", j=2, p=P, e=2),
-                    op=ALU.mult,
-                )
+                q, i = divmod(r, ROWS)
+                nc.vector.tensor_tensor(out=o_sb[r][:, c], in0=hh_ps[(r, s)][:], in1=h_sb[q][:, i, c], op=ALU.subtract)
 
         def store(r):
             q, i = divmod(r, ROWS)
@@ -262,7 +221,7 @@ def tile_tpru_pb_t_kernel(tc, a, vr, h, x2g, w_g, b_g, bg, out):
             return 0 <= r < NT
 
         with tc.manual_schedule():
-            for r in range(-K0, NT + 3):
+            for r in range(-TF, NT + 4):
                 if r >= -ROWS and r % ROWS == 0 and r // ROWS + 3 < GROUPS:
                     load_x(r // ROWS + 3)
                 if r >= -1 and r % ROWS == ROWS - 1 and (r + 9) // ROWS < GROUPS:
@@ -293,18 +252,18 @@ def tile_tpru_pb_t_kernel(tc, a, vr, h, x2g, w_g, b_g, bg, out):
                         d_close(r, s)
                 if (r + 2) % ROWS == 0 and ok(r + 2):
                     c_a((r + 2) // ROWS)
-                if ok(r + 2) and not is_x(r + 2):
-                    nh_make(r + 2)
                 if ok(r + K0):
                     p0(r + K0)
                 if ok(r + 2) and (r + 2) % 2 == 0:
                     quant(r + 2)
                 if ok(r - 1) and r - 1 < NT - 1:
                     q1, i1 = divmod(r - 1, ROWS)
+                    if not is_x(r - 1):
+                        nc.gpsimd.tensor_tensor(out=o_sb[r - 1][:], in0=o_sb[r - 1][:], in1=z_sb[r - 1][:], op=ALU.mult)
                     nc.gpsimd.tensor_tensor(out=o_sb[r - 1][:], in0=o_sb[r - 1][:], in1=h_sb[q1][:, i1, :], op=ALU.add)
                 if ok(r + TF):
                     t_h(r + TF)
                 if (r + 3) % ROWS == 0 and ok(r + 3):
                     t_a((r + 3) // ROWS)
-                if ok(r - 2) and r - 2 < NT - 1:
-                    store(r - 2)
+                if ok(r - 3) and r - 3 < NT - 1:
+                    store(r - 3)

@@ -17,22 +17,26 @@ DS = D // S
 ROWS = 4
 GROUPS = B // (P * ROWS)
 NT = GROUPS * ROWS
-K0 = 4
+K0 = 6
 TF = 5
 
 FLOPS = 2 * B * D * D + 2 * B * N * D
 
 
 def is_x(r):
-    return r % 2 == 1
+    return r % 2 == 0
+
+
+def p0_on_gpsimd(r):
+    return r >= 6 and r % 3 == 0
 
 
 def tile_tpru_pb_t_kernel(tc, a, vr, h, x2g, w_g, b_g, bg, out):
     nc = tc.nc
-    h_v = h.rearrange("(q p i) k -> q p i k", p=P, i=ROWS)
-    x_v = x2g.rearrange("(q p i) k -> q p i k", p=P, i=ROWS)
-    a_v = a.rearrange("(q p i) n s -> q p i (n s)", p=P, i=ROWS)
-    o_v = out.rearrange("(q p i) k -> q p i k", p=P, i=ROWS)
+    h_v = h.rearrange("(q i p) k -> q p i k", p=P, i=ROWS)
+    x_v = x2g.rearrange("(q i p) k -> q p i k", p=P, i=ROWS)
+    a_v = a.rearrange("(q i p) n s -> q p i (n s)", p=P, i=ROWS)
+    o_v = out.rearrange("(q i p) k -> q p i k", p=P, i=ROWS)
     w_v = w_g.rearrange("(j p) k -> p j k", p=P)
 
     with ExitStack() as ctx:
@@ -43,7 +47,7 @@ def tile_tpru_pb_t_kernel(tc, a, vr, h, x2g, w_g, b_g, bg, out):
         psb = ctx.enter_context(tc.psum_pool(name="psb", bufs=1))
 
         h_sb, x_sb, a_sb, aT_sb, tp_ps, ta_ps = {}, {}, {}, {}, {}, {}
-        hg_sb, hc_sb, hs_sb, acc_ps, hh_ps, z_sb, o_sb = {}, {}, {}, {}, {}, {}, {}
+        hg_sb, hc_sb, hs_sb, nh_sb, acc_ps, hh_ps, z_sb, o_sb = {}, {}, {}, {}, {}, {}, {}, {}
 
         def load_x(q):
             x_sb[q] = ld.tile([P, ROWS, D], BF16, name="x_t", tag="x")
@@ -73,6 +77,8 @@ def tile_tpru_pb_t_kernel(tc, a, vr, h, x2g, w_g, b_g, bg, out):
         wc = const.tile([P, 2, D], U32, name="wc", align_bytes=64)
         ws = const.tile([P, 2, D], U8, name="ws", align_bytes=64)
         vr_sb = const.tile([P, S, DS], BF16, name="vr_sb")
+        vrp_sb = const.tile([P, S, DS], BF16, name="vrp_sb")
+        bias_sb = const.tile([P, D], F32, name="bias_sb")
 
         wtmp = tc.tile_pool(name="wtmp", bufs=1)
         with wtmp as wt:
@@ -89,6 +95,11 @@ def tile_tpru_pb_t_kernel(tc, a, vr, h, x2g, w_g, b_g, bg, out):
             load_h(1)
             load_a(1)
 
+            nc.vector.tensor_copy(
+                out=vrp_sb[:].rearrange("n s (j e p) -> n (s j) e p", j=2, e=2, p=P),
+                in_=vr_sb[:].rearrange("n s (j p e) -> n (s j) e p", j=2, e=2, p=P),
+            )
+
             b_t = psum.tile([P, P], BF16, name="b_t", tag="tp")
             nc.tensor.transpose(b_t[:], brow[:], ident_b[:])
             bg_f = const.tile([P, 1], F32, name="bg_f")
@@ -102,6 +113,8 @@ def tile_tpru_pb_t_kernel(tc, a, vr, h, x2g, w_g, b_g, bg, out):
                 bias_ps.append(psb.tile([P, DS], F32, name="bias%d" % u))
             for j in range(8):
                 nc.tensor.transpose(bias_ps[j // 4][:, P * (j % 4) : P * (j % 4) + P], brep[:, j, :], ident_f[:])
+            for u in range(2):
+                nc.scalar.copy(out=bias_sb[:, DS * u : DS * u + DS], in_=bias_ps[u][:])
 
             wg = wt.tile([P, 2 * D * 4], BF16, name="wg", align_bytes=64)
             wg_f = wg[:].bitcast(F32).rearrange("p (g c u) -> p g c u", g=2, c=D, u=2)
@@ -152,6 +165,16 @@ def tile_tpru_pb_t_kernel(tc, a, vr, h, x2g, w_g, b_g, bg, out):
                 in_=hg_sb[q][:, i0 : i0 + 2, :].rearrange("p i x -> p (i x)"),
             )
 
+        def nh_make(r):
+            q, i = divmod(r, ROWS)
+            nh_sb[r] = late.tile([P, 2, 4, P], F32, name="nh", tag="nh")
+            for g in range(2):
+                nc.scalar.mul(
+                    out=nh_sb[r][:, g, :, :],
+                    in_=hg_sb[q][:, i, 4 * P * g : 4 * P * g + 4 * P].rearrange("p (r t) -> p t r", r=P, t=4),
+                    mul=-1.0,
+                )
+
         def t_a(q):
             ta_ps[q] = psum.tile([P, ROWS, P], F32, name="tpa", tag="tp")
             for i in range(ROWS):
@@ -166,7 +189,10 @@ def tile_tpru_pb_t_kernel(tc, a, vr, h, x2g, w_g, b_g, bg, out):
 
         def p0(r):
             q, i = divmod(r, ROWS)
-            z_sb[r] = work.tile([P, D], F32, name="z_t", tag="z", bufs=K0 + 5)
+            z_sb[r] = work.tile([P, D], F32, name="z_t", tag="z", bufs=K0 + 3)
+            if p0_on_gpsimd(r):
+                nc.gpsimd.tensor_tensor(out=z_sb[r][:], in0=x_sb[q][:, i, :], in1=bias_sb[:], op=ALU.add)
+                return
             for u in range(2):
                 c = slice(DS * u, DS * u + DS)
                 nc.vector.tensor_tensor(out=z_sb[r][:, c], in0=bias_ps[u][:], in1=x_sb[q][:, i, c], op=ALU.add)
@@ -194,7 +220,8 @@ def tile_tpru_pb_t_kernel(tc, a, vr, h, x2g, w_g, b_g, bg, out):
         def d_open(r, s):
             q, i = divmod(r, ROWS)
             hb = psum.tile([P, DS], F32, name="hb", tag="hh")
-            nc.tensor.matmul(out=hb[:], lhsT=aT_sb[q][:, i, s, :], rhs=vr_sb[:, s, :], start=True, stop=not is_x(r))
+            rhs = vr_sb if is_x(r) else vrp_sb
+            nc.tensor.matmul(out=hb[:], lhsT=aT_sb[q][:, i, s, :], rhs=rhs[:, s, :], start=True, stop=False)
             hh_ps[(r, s)] = hb
 
         def d_close(r, s):
@@ -202,16 +229,30 @@ def tile_tpru_pb_t_kernel(tc, a, vr, h, x2g, w_g, b_g, bg, out):
             hb = hh_ps[(r, s)]
             if is_x(r):
                 nc.tensor.matmul(out=hb[:], lhsT=neg_i[:], rhs=h_sb[q][:, i, DS * s : DS * s + DS], start=False, stop=True)
+                return
+            for t in range(4):
+                nc.tensor.matmul(
+                    out=hb[:, P * t : P * t + P],
+                    lhsT=nh_sb[r][:, s, t, :],
+                    rhs=ident_f[:],
+                    start=False,
+                    stop=(t == 3),
+                    is_transpose=True,
+                )
 
         def p4(r, s):
             c = slice(DS * s, DS * s + DS)
             if s == 0:
-                o_sb[r] = late.tile([P, D], F32, name="o_t", tag="o", bufs=7)
+                o_sb[r] = late.tile([P, D], F32, name="o_t", tag="o", bufs=6)
             if is_x(r):
                 nc.vector.tensor_tensor(out=o_sb[r][:, c], in0=hh_ps[(r, s)][:], in1=z_sb[r][:, c], op=ALU.mult)
             else:
-                q, i = divmod(r, ROWS)
-                nc.vector.tensor_tensor(out=o_sb[r][:, c], in0=hh_ps[(r, s)][:], in1=h_sb[q][:, i, c], op=ALU.subtract)
+                nc.vector.tensor_tensor(
+                    out=o_sb[r][:, c].rearrange("r (j p e) -> r j p e", j=2, p=P, e=2),
+                    in0=hh_ps[(r, s)][:].rearrange("r (j e p) -> r j p e", j=2, p=P, e=2),
+                    in1=z_sb[r][:, c].rearrange("r (j p e) -> r j p e", j=2, p=P, e=2),
+                    op=ALU.mult,
+                )
 
         def store(r):
             q, i = divmod(r, ROWS)
@@ -221,7 +262,7 @@ def tile_tpru_pb_t_kernel(tc, a, vr, h, x2g, w_g, b_g, bg, out):
             return 0 <= r < NT
 
         with tc.manual_schedule():
-            for r in range(-TF, NT + 4):
+            for r in range(-K0, NT + 3):
                 if r >= -ROWS and r % ROWS == 0 and r // ROWS + 3 < GROUPS:
                     load_x(r // ROWS + 3)
                 if r >= -1 and r % ROWS == ROWS - 1 and (r + 9) // ROWS < GROUPS:
@@ -252,18 +293,18 @@ def tile_tpru_pb_t_kernel(tc, a, vr, h, x2g, w_g, b_g, bg, out):
                         d_close(r, s)
                 if (r + 2) % ROWS == 0 and ok(r + 2):
                     c_a((r + 2) // ROWS)
+                if ok(r + 2) and not is_x(r + 2):
+                    nh_make(r + 2)
                 if ok(r + K0):
                     p0(r + K0)
                 if ok(r + 2) and (r + 2) % 2 == 0:
                     quant(r + 2)
                 if ok(r - 1) and r - 1 < NT - 1:
                     q1, i1 = divmod(r - 1, ROWS)
-                    if not is_x(r - 1):
-                        nc.gpsimd.tensor_tensor(out=o_sb[r - 1][:], in0=o_sb[r - 1][:], in1=z_sb[r - 1][:], op=ALU.mult)
                     nc.gpsimd.tensor_tensor(out=o_sb[r - 1][:], in0=o_sb[r - 1][:], in1=h_sb[q1][:, i1, :], op=ALU.add)
                 if ok(r + TF):
                     t_h(r + TF)
                 if (r + 3) % ROWS == 0 and ok(r + 3):
                     t_a((r + 3) // ROWS)
-                if ok(r - 3) and r - 3 < NT - 1:
-                    store(r - 3)
+                if ok(r - 2) and r - 2 < NT - 1:
+                    store(r - 2)

@@ -28,15 +28,15 @@ def is_x(r):
 
 
 def p0_on_gpsimd(r):
-    return r >= 6 and r % 3 == 0
+    return r >= 6 and r % 2 == 0 and r % 8 != 4
 
 
 def tile_tpru_pb_t_kernel(tc, a, vr, h, x2g, w_g, b_g, bg, out):
     nc = tc.nc
-    h_v = h.rearrange("(q i p) k -> q p i k", p=P, i=ROWS)
-    x_v = x2g.rearrange("(q i p) k -> q p i k", p=P, i=ROWS)
-    a_v = a.rearrange("(q i p) n s -> q p i (n s)", p=P, i=ROWS)
-    o_v = out.rearrange("(q i p) k -> q p i k", p=P, i=ROWS)
+    h_v = h.rearrange("(q p i) k -> q p i k", p=P, i=ROWS)
+    x_v = x2g.rearrange("(q p i) k -> q p i k", p=P, i=ROWS)
+    a_v = a.rearrange("(q p i) n s -> q p i (n s)", p=P, i=ROWS)
+    o_v = out.rearrange("(q p i) k -> q p i k", p=P, i=ROWS)
     w_v = w_g.rearrange("(j p) k -> p j k", p=P)
 
     with ExitStack() as ctx:
@@ -297,8 +297,8 @@ def tile_tpru_pb_t_kernel(tc, a, vr, h, x2g, w_g, b_g, bg, out):
                     nh_make(r + 2)
                 if ok(r + K0):
                     p0(r + K0)
-                if ok(r + 2) and (r + 2) % 2 == 0:
-                    quant(r + 2)
+                if ok(r + 3) and (r + 3) % 2 == 0:
+                    quant(r + 3)
                 if ok(r - 1) and r - 1 < NT - 1:
                     q1, i1 = divmod(r - 1, ROWS)
                     nc.gpsimd.tensor_tensor(out=o_sb[r - 1][:], in0=o_sb[r - 1][:], in1=h_sb[q1][:, i1, :], op=ALU.add)

from contextlib import ExitStack

import concourse.mybir as mybir
from concourse.masks import make_identity

F32 = mybir.dt.float32
BF16 = mybir.dt.bfloat16
U32 = mybir.dt.uint32
U8 = mybir.dt.uint8
FP8X4 = mybir.dt.float8_e4m3fn_x4
ALU = mybir.AluOpType
ACT = mybir.ActivationFunctionType

P = 128
B, D, S, N = 4096, 1024, 2, 128
DS = D // S
ROWS = 4
GROUPS = B // (P * ROWS)
NT = GROUPS * ROWS
K0 = 6
TF = 5

FLOPS = 2 * B * D * D + 2 * B * N * D


def is_x(r):
    return r % 2 == 0


def p0_on_gpsimd(r):
    return r >= 6 and r % 2 == 0 and r % 8 != 4


def tile_tpru_pb_t_kernel(tc, a, vr, h, x2g, w_g, b_g, bg, out):
    nc = tc.nc
    h_v = h.rearrange("(q p i) k -> q p i k", p=P, i=ROWS)
    x_v = x2g.rearrange("(q p i) k -> q p i k", p=P, i=ROWS)
    a_v = a.rearrange("(q p i) n s -> q p i (n s)", p=P, i=ROWS)
    o_v = out.rearrange("(q p i) k -> q p i k", p=P, i=ROWS)
    w_v = w_g.rearrange("(j p) k -> p j k", p=P)

    with ExitStack() as ctx:
        const = ctx.enter_context(tc.tile_pool(name="const", bufs=1))
        ld = ctx.enter_context(tc.tile_pool(name="ld", bufs=3))
        work = ctx.enter_context(tc.tile_pool(name="work", bufs=2))
        psum = ctx.enter_context(tc.psum_pool(name="psum", bufs=2))
        psb = ctx.enter_context(tc.psum_pool(name="psb", bufs=1))

        h_sb, x_sb, a_sb, aT_sb, tp_ps, ta_ps = {}, {}, {}, {}, {}, {}
        hg_sb, hc_sb, hs_sb, nh_sb, acc_ps, hh_ps, z_sb, o_sb = {}, {}, {}, {}, {}, {}, {}, {}

        def load_x(q):
            x_sb[q] = ld.tile([P, ROWS, D], BF16, name="x_t", tag="x")
            nc.sync.dma_start(out=x_sb[q][:], in_=x_v[q])

        def load_h(q):
            h_sb[q] = ld.tile([P, ROWS, D], BF16, name="h_t", tag="h", bufs=4)
            nc.sync.dma_start(out=h_sb[q][:], in_=h_v[q])

        def load_a(q):
            a_sb[q] = ld.tile([P, ROWS, 2 * N], BF16, name="a_t", tag="a")
            nc.sync.dma_start(out=a_sb[q][:], in_=a_v[q])

        ident_f = const.tile([P, P], F32, name="ident_f")
        make_identity(nc, ident_f[:])
        ident_b = const.tile([P, P], BF16, name="ident_b")
        make_identity(nc, ident_b[:])
        neg_i = const.tile([P, P], BF16, name="neg_i")
        nc.vector.tensor_scalar_mul(out=neg_i[:], in0=ident_b[:], scalar1=-1.0)

        brow = const.tile([P, P], BF16, name="brow")
        nc.vector.memset(brow[:], 0.0)
        nc.sync.dma_start(out=brow[0:8, :], in_=b_g.rearrange("(j c) -> j c", c=P))
        bg_b = const.tile([P, 1], BF16, name="bg_b")
        nc.sync.dma_start(out=bg_b[:], in_=bg.partition_broadcast(P))

        wc = const.tile([P, 2, D], U32, name="wc", align_bytes=64)
        ws = const.tile([P, 2, D], U8, name="ws", align_bytes=64)
        vr_sb = const.tile([P, S, DS], BF16, name="vr_sb")
        vrp_sb = const.tile([P, S, DS], BF16, name="vrp_sb")
        bias_sb = const.tile([P, D], F32, name="bias_sb")

        wtmp = tc.tile_pool(name="wtmp", bufs=1)
        with wtmp as wt:
            load_x(0)
            wraw = wt.tile([P, 8, D], BF16, name="wraw")
            nc.sync.dma_start(out=wraw[:, 0:4, :], in_=w_v[:, 0:4, :])
            h_sb[0] = ld.tile([P, ROWS, D], BF16, name="h_t", tag="h", bufs=4)
            nc.sync.dma_start(out=h_sb[0][:, 0:1, :], in_=h_v[0][:, 0:1, :])
            nc.sync.dma_start(out=wraw[:, 4:8, :], in_=w_v[:, 4:8, :])
            load_a(0)
            nc.sync.dma_start(out=vr_sb[:], in_=vr)
            nc.sync.dma_start(out=h_sb[0][:, 1:4, :], in_=h_v[0][:, 1:4, :])
            load_x(1)
            load_h(1)
            load_a(1)

            nc.vector.tensor_copy(
                out=vrp_sb[:].rearrange("n s (j e p) -> n (s j) e p", j=2, e=2, p=P),
                in_=vr_sb[:].rearrange("n s (j p e) -> n (s j) e p", j=2, e=2, p=P),
            )

            b_t = psum.tile([P, P], BF16, name="b_t", tag="tp")
            nc.tensor.transpose(b_t[:], brow[:], ident_b[:])
            bg_f = const.tile([P, 1], F32, name="bg_f")
            nc.vector.tensor_copy(out=bg_f[:], in_=bg_b[:])
            bcol = const.tile([P, 8], F32, name="bcol")
            nc.vector.tensor_scalar_add(out=bcol[:], in0=b_t[:, 0:8], scalar1=bg_f[:, 0:1])
            brep = wt.tile([P, 8, P], F32, name="brep")
            nc.vector.tensor_copy(out=brep[:], in_=bcol[:].unsqueeze(2).to_broadcast([P, 8, P]))
            bias_ps = []
            for u in range(2):
                bias_ps.append(psb.tile([P, DS], F32, name="bias%d" % u))
            for j in range(8):
                nc.tensor.transpose(bias_ps[j // 4][:, P * (j % 4) : P * (j % 4) + P], brep[:, j, :], ident_f[:])
            for u in range(2):
                nc.scalar.copy(out=bias_sb[:, DS * u : DS * u + DS], in_=bias_ps[u][:])

            wg = wt.tile([P, 2 * D * 4], BF16, name="wg", align_bytes=64)
            wg_f = wg[:].bitcast(F32).rearrange("p (g c u) -> p g c u", g=2, c=D, u=2)
            wg_q = wg[:].rearrange("p (g x) -> p g x", g=2)
            for j in range(8):
                tpw = psum.tile([P, 4, P], F32, name="tpw", tag="tp")
                wj = wraw[:, j, :].bitcast(F32)
                for blk in range(4):
                    nc.tensor.transpose(tpw[:, blk, :], wj[:, P * blk : P * blk + P], ident_f[:])
                nc.scalar.copy(
                    out=wg_f[:, :, P * j : P * j + P, :],
                    in_=tpw[:].rearrange("p (g u) r -> p g r u", g=2, u=2),
                )
                if j % 4 == 3:
                    u = j // 4
                    for g in range(2):
                        nc.vector.quantize_mx(
                            out=wc[:, g, DS * u : DS * u + DS].bitcast(FP8X4),
                            scales=ws[:, g, DS * u : DS * u + DS],
                            in_=wg_q[:, g, 4 * DS * u : 4 * DS * u + 4 * DS],
                        )

        late = ctx.enter_context(tc.tile_pool(name="late", bufs=3))

        def t_h(r):
            q, i = divmod(r, ROWS)
            tp_ps[r] = psum.tile([P, 4, P], F32, name="tph", tag="tp")
            hw = h_sb[q][:, i, :].bitcast(F32)
            for blk in range(4):
                nc.tensor.transpose(tp_ps[r][:, blk, :], hw[:, P * blk : P * blk + P], ident_f[:])

        def c_h(r):
            q, i = divmod(r, ROWS)
            if i == 0:
                hg_sb[q] = work.tile([P, ROWS, D], BF16, name="hg", tag="hg", align_bytes=64)
                hc_sb[q] = work.tile([P, ROWS, 2, P], U32, name="hc", tag="hc", align_bytes=64)
                hs_sb[q] = work.tile([P, ROWS, 2, P], U8, name="hs", tag="hs", align_bytes=64)
            nc.scalar.copy(
                out=hg_sb[q][:, i, :].bitcast(F32).rearrange("p (g r u) -> p g r u", g=2, r=P, u=2),
                in_=tp_ps[r][:].rearrange("p (g u) r -> p g r u", g=2, u=2),
            )

        def quant(r0):
            q, i0 = divmod(r0, ROWS)
            nc.vector.quantize_mx(
                out=hc_sb[q][:, i0 : i0 + 2, :, :].rearrange("p i g r -> p (i g r)").bitcast(FP8X4),
                scales=hs_sb[q][:, i0 : i0 + 2, :, :].rearrange("p i g r -> p (i g r)"),
                in_=hg_sb[q][:, i0 : i0 + 2, :].rearrange("p i x -> p (i x)"),
            )

        def nh_make(r):
            q, i = divmod(r, ROWS)
            nh_sb[r] = late.tile([P, 2, 4, P], F32, name="nh", tag="nh")
            for g in range(2):
                nc.scalar.mul(
                    out=nh_sb[r][:, g, :, :],
                    in_=hg_sb[q][:, i, 4 * P * g : 4 * P * g + 4 * P].rearrange("p (r t) -> p t r", r=P, t=4),
                    mul=-1.0,
                )

        def t_a(q):
            ta_ps[q] = psum.tile([P, ROWS, P], F32, name="tpa", tag="tp")
            for i in range(ROWS):
                nc.tensor.transpose(ta_ps[q][:, i, :], a_sb[q][:, i, :].bitcast(F32), ident_f[:])

        def c_a(q):
            aT_sb[q] = work.tile([P, ROWS, S, P], BF16, name="aT", tag="aT")
            nc.scalar.copy(
                out=aT_sb[q][:],
                in_=ta_ps[q][:].rearrange("p i b -> p (i b)").bitcast(BF16).rearrange("p (i b s) -> p i s b", i=ROWS, b=P, s=S),
            )

        def p0(r):
            q, i = divmod(r, ROWS)
            z_sb[r] = work.tile([P, D], F32, name="z_t", tag="z", bufs=K0 + 3)
            if p0_on_gpsimd(r):
                nc.gpsimd.tensor_tensor(out=z_sb[r][:], in0=x_sb[q][:, i, :], in1=bias_sb[:], op=ALU.add)
                return
            for u in range(2):
                c = slice(DS * u, DS * u + DS)
                nc.vector.tensor_tensor(out=z_sb[r][:, c], in0=bias_ps[u][:], in1=x_sb[q][:, i, c], op=ALU.add)

        def mm(r, u):
            q, i = divmod(r, ROWS)
            c = slice(DS * u, DS * u + DS)
            acc = psum.tile([P, DS], F32, name="acc", tag="h2g")
            for g in range(2):
                nc.tensor.matmul_mx(
                    out=acc[:],
                    lhsT=hc_sb[q][:, i, g, :].bitcast(FP8X4),
                    lhsT_scale=hs_sb[q][:, i, g, :],
                    rhs=wc[:, g, c].bitcast(FP8X4),
                    rhs_scale=ws[:, g, c],
                    start=(g == 0),
                    stop=(g == 1),
                )
            acc_ps[(r, u)] = acc

        def p1(r, u):
            c = slice(DS * u, DS * u + DS)
            nc.vector.tensor_tensor(out=z_sb[r][:, c], in0=acc_ps[(r, u)][:], in1=z_sb[r][:, c], op=ALU.add)

        def d_open(r, s):
            q, i = divmod(r, ROWS)
            hb = psum.tile([P, DS], F32, name="hb", tag="hh")
            rhs = vr_sb if is_x(r) else vrp_sb
            nc.tensor.matmul(out=hb[:], lhsT=aT_sb[q][:, i, s, :], rhs=rhs[:, s, :], start=True, stop=False)
            hh_ps[(r, s)] = hb

        def d_close(r, s):
            q, i = divmod(r, ROWS)
            hb = hh_ps[(r, s)]
            if is_x(r):
                nc.tensor.matmul(out=hb[:], lhsT=neg_i[:], rhs=h_sb[q][:, i, DS * s : DS * s + DS], start=False, stop=True)
                return
            for t in range(4):
                nc.tensor.matmul(
                    out=hb[:, P * t : P * t + P],
                    lhsT=nh_sb[r][:, s, t, :],
                    rhs=ident_f[:],
                    start=False,
                    stop=(t == 3),
                    is_transpose=True,
                )

        def p4(r, s):
            c = slice(DS * s, DS * s + DS)
            if s == 0:
                o_sb[r] = late.tile([P, D], F32, name="o_t", tag="o", bufs=6)
            if is_x(r):
                nc.vector.tensor_tensor(out=o_sb[r][:, c], in0=hh_ps[(r, s)][:], in1=z_sb[r][:, c], op=ALU.mult)
            else:
                nc.vector.tensor_tensor(
                    out=o_sb[r][:, c].rearrange("r (j p e) -> r j p e", j=2, p=P, e=2),
                    in0=hh_ps[(r, s)][:].rearrange("r (j e p) -> r j p e", j=2, p=P, e=2),
                    in1=z_sb[r][:, c].rearrange("r (j p e) -> r j p e", j=2, p=P, e=2),
                    op=ALU.mult,
                )

        def store(r):
            q, i = divmod(r, ROWS)
            nc.sync.dma_start(out=o_v[q][:, i, :], in_=o_sb[r][:])

        def ok(r):
            return 0 <= r < NT

        with tc.manual_schedule():
            for r in range(-K0, NT + 3):
                if r >= -ROWS and r % ROWS == 0 and r // ROWS + 3 < GROUPS:
                    load_x(r // ROWS + 3)
                if r >= -1 and r % ROWS == ROWS - 1 and (r + 9) // ROWS < GROUPS:
                    load_h((r + 9) // ROWS)
                    load_a((r + 9) // ROWS)
                for u in range(2):
                    if ok(r):
                        p1(r, u)
                    if ok(r + 1):
                        mm(r + 1, u)
                if ok(r):
                    nc.scalar.activation(out=z_sb[r][:], in_=z_sb[r][:], func=ACT.Sigmoid)
                if ok(r + 4):
                    c_h(r + 4)
                if ok(r - 1):
                    for s in range(S):
                        p4(r - 1, s)
                        if r - 1 == NT - 1:
                            c = slice(DS * s, DS * s + DS)
                            nc.vector.tensor_tensor(
                                out=o_sb[r - 1][:, c], in0=o_sb[r - 1][:, c], in1=h_sb[GROUPS - 1][:, ROWS - 1, c], op=ALU.add
                            )
                            nc.sync.dma_start(out=o_v[GROUPS - 1][:, ROWS - 1, c], in_=o_sb[r - 1][:, c])
                if ok(r):
                    for s in range(S):
                        d_open(r, s)
                    for s in range(S):
                        d_close(r, s)
                if (r + 2) % ROWS == 0 and ok(r + 2):
                    c_a((r + 2) // ROWS)
                if ok(r + 2) and not is_x(r + 2):
                    nh_make(r + 2)
                if ok(r + K0):
                    p0(r + K0)
                if ok(r + 3) and (r + 3) % 2 == 0:
                    quant(r + 3)
                if ok(r - 1) and r - 1 < NT - 1:
                    q1, i1 = divmod(r - 1, ROWS)
                    nc.gpsimd.tensor_tensor(out=o_sb[r - 1][:], in0=o_sb[r - 1][:], in1=h_sb[q1][:, i1, :], op=ALU.add)
                if ok(r + TF):
                    t_h(r + TF)
                if (r + 3) % ROWS == 0 and ok(r + 3):
                    t_a((r + 3) // ROWS)
                if ok(r - 2) and r - 2 < NT - 1:
                    store(r - 2)
